import numpy as np
import ml_dtypes


def mxq(x, axis, fmt="e4m3"):
    dtype, down = {"e4m3": (ml_dtypes.float8_e4m3fn, 7), "e5m2": (ml_dtypes.float8_e5m2, 14)}[fmt]
    v = np.moveaxis(np.asarray(x, np.float32).astype(ml_dtypes.bfloat16).astype(np.float64), axis, -1)
    blocks = v.reshape(v.shape[:-1] + (-1, 32))
    amax = np.abs(blocks).max(-1, keepdims=True)
    byte = np.maximum(np.where(amax > 0, np.frexp(amax)[1] - 1 + 127, 0) - down, 1)
    scale = np.exp2(byte - 127.0)
    codes = (blocks / scale).astype(np.float32).astype(dtype).astype(np.float64)
    return np.moveaxis((codes * scale).reshape(v.shape), -1, axis)


WIDE = False


def mx_kscale(k):
    if not WIDE:
        return np.ones(k)
    levels = np.array([10, -10, 5, -5, 0])
    a = np.random.permutation(np.resize(levels, k // 512 * 4)).reshape(k // 512, 4)
    idx = np.arange(k)
    return np.exp2(a[idx // 512, idx % 128 // 32])


BF16 = ml_dtypes.bfloat16


def bf(x):
    return np.asarray(x, np.float32).astype(BF16)


def f64(x):
    return np.asarray(x).astype(np.float64)


B, N, E, H, G, C, EO = 4, 2048, 512, 8, 128, 512, 128
LN_EPS = 1e-5


def sigmoid(v):
    return 1.0 / (1.0 + np.exp(-v))


def layernorm(y, w, b):
    mu = y.mean(-1, keepdims=True)
    var = np.square(y - mu).mean(-1, keepdims=True)
    return (y - mu) / np.sqrt(var + LN_EPS) * w + b


def setup_inputs():
    s = mx_kscale(E)
    return {"attn": bf((1.5 + 2.5 * np.random.standard_normal((B, N, E))) * s),
            "gate_low": bf(np.random.standard_normal((B, N, G))),
            "Wg2": bf(np.random.standard_normal((G, E)) / np.sqrt(G)),
            "Wo": bf(np.random.standard_normal((E, EO)) / np.sqrt(E) / s[:, None]),
            "ln_w": bf(1.0 + 0.1 * np.random.standard_normal(EO)),
            "ln_b": bf(0.1 * np.random.standard_normal(EO))}


def reference(attn, gate_low, Wg2, Wo, ln_w, ln_b):
    gate = sigmoid(f64(gate_low) @ f64(Wg2))
    h = f64(attn) * gate
    y = mxq(h, 2, "e4m3") @ mxq(f64(Wo), 0, "e4m3")
    return layernorm(y, f64(ln_w), f64(ln_b))

@@ -1,0 +1,228 @@
+from contextlib import ExitStack
+
+import concourse.mybir as mybir
+from concourse.masks import make_identity
+
+F32 = mybir.dt.float32
+BF16 = mybir.dt.bfloat16
+U32 = mybir.dt.uint32
+U8 = mybir.dt.uint8
+FP8X4 = mybir.dt.float8_e4m3fn_x4
+ACT = mybir.ActivationFunctionType
+ALU = mybir.AluOpType
+
+P = 128
+PACK = 4
+TOKENS = 4 * 2048
+E = 512
+G = 128
+EO = 128
+LN_EPS = 1e-5
+
+PAIR_TILES = 2
+QUAD_TILES = 4
+CHUNK_TILES = 8
+PAIR = PAIR_TILES * P
+CHUNK = CHUNK_TILES * P
+N_CHUNKS = TOKENS // CHUNK
+N_PAIRS = TOKENS // PAIR
+PAIRS_PER_CHUNK = CHUNK_TILES // PAIR_TILES
+PAIRS_PER_QUAD = QUAD_TILES // PAIR_TILES
+BN_STATS = 6
+BN_AGGR = 2
+
+FLOPS = 2 * TOKENS * G * E + 2 * TOKENS * E * EO
+
+
+def tile_tnlattention_pb_t_kernel(tc, attn, gate_low, Wg2, Wo, ln_w, ln_b, out):
+    nc = tc.nc
+    attn_rows = attn.flatten_outer_dims()
+    gate_low_rows = gate_low.flatten_outer_dims()
+    out_rows = out.flatten_outer_dims()
+
+    with ExitStack() as ctx:
+        consts = ctx.enter_context(tc.tile_pool(name="consts", bufs=1))
+        attn_pool = ctx.enter_context(tc.tile_pool(name="attn", bufs=N_CHUNKS))
+        gate_low_pool = ctx.enter_context(tc.tile_pool(name="gate_low", bufs=N_CHUNKS))
+        gate_low_t_pool = ctx.enter_context(tc.tile_pool(name="gate_low_t", bufs=2))
+        gate_pool = ctx.enter_context(tc.tile_pool(name="gate", bufs=3))
+        h_pool = ctx.enter_context(tc.tile_pool(name="h", bufs=3))
+        mx_pool = ctx.enter_context(tc.tile_pool(name="mx", bufs=3))
+        stat_pool = ctx.enter_context(tc.tile_pool(name="stat", bufs=4))
+        result_pool = ctx.enter_context(tc.tile_pool(name="result", bufs=6))
+        gate_low_t_psum = ctx.enter_context(tc.psum_pool(name="gate_low_t_ps", bufs=1))
+        attn_t_psum = ctx.enter_context(tc.psum_pool(name="attn_t_ps", bufs=2))
+        z_psum = ctx.enter_context(tc.psum_pool(name="z_ps", bufs=3))
+        y_psum = ctx.enter_context(tc.psum_pool(name="y_ps", bufs=2))
+
+        attn_chunks = []
+        gate_low_chunks = []
+
+        def load_chunk(c):
+            rows = slice(c * CHUNK, (c + 1) * CHUNK)
+            gate_low_sb = gate_low_pool.tile([P, CHUNK_TILES, G], BF16)
+            nc.sync.dma_start(
+                out=gate_low_sb[:],
+                in_=gate_low_rows[rows, :].rearrange("(p j) g -> p j g", j=CHUNK_TILES),
+            )
+            gate_low_chunks.append(gate_low_sb)
+            attn_sb = attn_pool.tile([P, CHUNK_TILES, E], BF16)
+            nc.sync.dma_start(
+                out=attn_sb[:],
+                in_=attn_rows[rows, :].rearrange("(p j) k -> p j k", j=CHUNK_TILES),
+            )
+            attn_chunks.append(attn_sb)
+
+        wg2_sb = consts.tile([P, E], BF16)
+        nc.sync.dma_start(out=wg2_sb[:], in_=Wg2[:, :])
+        load_chunk(0)
+        wo_rows = consts.tile([P, PACK, EO], BF16)
+        nc.sync.dma_start(
+            out=wo_rows[:].rearrange("q (u e) o -> q u (e o)", e=2),
+            in_=Wo.rearrange("(u q e) o -> q u (e o)", u=2, e=2),
+        )
+        ln_w_all = consts.tile([P, EO], BF16)
+        nc.sync.dma_start(out=ln_w_all[:], in_=ln_w.partition_broadcast(P))
+        ln_b_all = consts.tile([P, EO], BF16)
+        nc.sync.dma_start(out=ln_b_all[:], in_=ln_b.partition_broadcast(P))
+        for c in range(1, N_CHUNKS):
+            load_chunk(c)
+
+        ident_bf16 = consts.tile([P, P], BF16)
+        make_identity(nc, ident_bf16[:])
+        ident_f32 = consts.tile([P, P], F32)
+        make_identity(nc, ident_f32[:])
+        minus_half = consts.tile([P, QUAD_TILES], F32)
+        nc.vector.memset(minus_half[:], -0.5)
+        warm = consts.tile([P, 1], F32)
+        nc.vector.memset(warm[:], 0.0)
+        nc.scalar.activation(out=warm[:], in_=warm[:], func=ACT.Sigmoid)
+
+        wg2_by_t = consts.tile([P, PACK, P], BF16)
+        nc.vector.tensor_copy(
+            out=wg2_by_t[:].rearrange("g (u e) q -> g u e q", e=2),
+            in_=wg2_sb[:].rearrange("g (u q e) -> g u e q", u=2, e=2),
+        )
+
+        wo_grouped = consts.tile([P, EO, PACK], BF16, align_bytes=64)
+        nc.vector.tensor_copy(out=wo_grouped[:], in_=wo_rows[:].rearrange("q t o -> q o t"))
+        wo_codes = consts.tile([P, EO], U32, align_bytes=64)
+        wo_scales = consts.tile([P, EO], U8, align_bytes=64)
+        nc.vector.quantize_mx(
+            out=wo_codes[:].bitcast(FP8X4),
+            scales=wo_scales[:],
+            in_=wo_grouped[:].rearrange("q o t -> q (o t)"),
+        )
+
+        def transpose_gate_low(c):
+            gate_low_t_ps = gate_low_t_psum.tile([P, CHUNK], BF16)
+            for j in range(CHUNK_TILES):
+                nc.tensor.transpose(
+                    gate_low_t_ps[:, j * P : (j + 1) * P], gate_low_chunks[c][:, j, :], ident_bf16[:]
+                )
+            gate_low_t = gate_low_t_pool.tile([P, CHUNK], BF16)
+            nc.scalar.copy(out=gate_low_t[:], in_=gate_low_t_ps[:])
+            return gate_low_t
+
+        def gated_product(s, gate_low_t):
+            c = s // PAIRS_PER_CHUNK
+            first_tile = (s % PAIRS_PER_CHUNK) * PAIR_TILES
+            attn_t_ps = attn_t_psum.tile([P, 2, PAIR], F32)
+            for i in range(PAIR_TILES):
+                words = attn_chunks[c][:, first_tile + i, :].bitcast(F32)
+                for u in range(2):
+                    nc.tensor.transpose(
+                        attn_t_ps[:, u, i * P : (i + 1) * P], words[:, u * P : (u + 1) * P], ident_f32[:]
+                    )
+            gate_sb = gate_pool.tile([P, PAIR, PACK], F32)
+            for i in range(PAIR_TILES):
+                tokens = slice((first_tile + i) * P, (first_tile + i + 1) * P)
+                z_ps = z_psum.tile([P, PACK, P], F32)
+                for t in range(PACK):
+                    nc.tensor.matmul(
+                        out=z_ps[:, t, :], lhsT=wg2_by_t[:, t, :], rhs=gate_low_t[:, tokens],
+                        start=True, stop=True,
+                    )
+                nc.scalar.activation(
+                    out=gate_sb[:, i * P : (i + 1) * P, :],
+                    in_=z_ps[:].rearrange("q t n -> q n t"),
+                    func=ACT.Sigmoid,
+                )
+            h_sb = h_pool.tile([P, PAIR, PACK], BF16, align_bytes=64)
+            nc.vector.tensor_tensor(
+                out=h_sb[:].rearrange("q n (u e) -> q n u e", e=2),
+                in0=attn_t_ps[:].bitcast(BF16).rearrange("q u (n e) -> q n u e", e=2),
+                in1=gate_sb[:].rearrange("q n (u e) -> q n u e", e=2),
+                op=ALU.mult,
+            )
+            return h_sb
+
+        def project(h_sb, y_ps, first_slot):
+            h_codes = mx_pool.tile([P, PAIR], U32, align_bytes=64)
+            h_scales = mx_pool.tile([P, PAIR], U8, align_bytes=64)
+            nc.vector.quantize_mx(
+                out=h_codes[:].bitcast(FP8X4),
+                scales=h_scales[:],
+                in_=h_sb[:].rearrange("q n t -> q (n t)"),
+            )
+            for i in range(PAIR_TILES):
+                tokens = slice(i * P, (i + 1) * P)
+                nc.tensor.matmul_mx(
+                    out=y_ps[:, first_slot + i, :],
+                    lhsT=h_codes[:, tokens].bitcast(FP8X4),
+                    lhsT_scale=h_scales[:, tokens],
+                    rhs=wo_codes[:].bitcast(FP8X4),
+                    rhs_scale=wo_scales[:],
+                    start=True,
+                    stop=True,
+                )
+
+        def layer_norm_and_store(quad, y_ps):
+            stats = stat_pool.tile([P, QUAD_TILES, BN_STATS], F32)
+            mean_var = stat_pool.tile([P, QUAD_TILES, BN_AGGR], F32)
+            for i in range(QUAD_TILES):
+                nc.vector.bn_stats(out=stats[:, i, :], in_=y_ps[:, i, :])
+            for i in range(QUAD_TILES):
+                nc.vector.bn_aggr(out=mean_var[:, i, :], in_=stats[:, i, :])
+            var_eps = stat_pool.tile([P, QUAD_TILES], F32)
+            nc.vector.tensor_scalar_add(out=var_eps[:], in0=mean_var[:, :, 1], scalar1=LN_EPS)
+            rstd = stat_pool.tile([P, QUAD_TILES], F32)
+            nc.gpsimd.tensor_tensor(out=rstd[:], in0=var_eps[:], in1=minus_half[:], op=ALU.pow)
+            shift = stat_pool.tile([P, QUAD_TILES], F32)
+            nc.vector.scalar_tensor_tensor(
+                out=shift[:], in0=mean_var[:, :, 0], scalar=-1.0, in1=rstd[:], op0=ALU.mult, op1=ALU.mult
+            )
+            result = result_pool.tile([P, QUAD_TILES, EO], F32)
+            for i in range(QUAD_TILES):
+                nc.scalar.activation(
+                    out=result[:, i, :], in_=y_ps[:, i, :], func=ACT.Identity,
+                    bias=shift[:, i : i + 1], scale=rstd[:, i : i + 1],
+                )
+            whole = [P, QUAD_TILES, EO]
+            nc.gpsimd.tensor_tensor(
+                out=result[:], in0=result[:], in1=ln_w_all[:].unsqueeze(1).to_broadcast(whole), op=ALU.mult
+            )
+            nc.gpsimd.tensor_tensor(
+                out=result[:], in0=result[:], in1=ln_b_all[:].unsqueeze(1).to_broadcast(whole), op=ALU.add
+            )
+            c = quad * QUAD_TILES // CHUNK_TILES
+            first_tile = quad * QUAD_TILES % CHUNK_TILES
+            chunk_rows = out_rows[c * CHUNK : (c + 1) * CHUNK, :].rearrange("(p j) o -> p j o", j=CHUNK_TILES)
+            nc.sync.dma_start(out=chunk_rows[:, first_tile : first_tile + QUAD_TILES, :], in_=result[:])
+
+        h_tiles = []
+        gate_low_t = None
+        y_ps = None
+        for s in range(N_PAIRS + 1):
+            if s < N_PAIRS:
+                if s % PAIRS_PER_CHUNK == 0:
+                    gate_low_t = transpose_gate_low(s // PAIRS_PER_CHUNK)
+                h_tiles.append(gated_product(s, gate_low_t))
+            if s >= 1:
+                done = s - 1
+                slot = done % PAIRS_PER_QUAD
+                if slot == 0:
+                    y_ps = y_psum.tile([P, QUAD_TILES, EO], F32)
+                project(h_tiles[done], y_ps, slot * PAIR_TILES)
+                if slot == PAIRS_PER_QUAD - 1:
+                    layer_norm_and_store(done // PAIRS_PER_QUAD, y_ps)

@@ -23,13 +23,24 @@ PAIR_TILES = 2
 QUAD_TILES = 4
 CHUNK_TILES = 8
 PAIR = PAIR_TILES * P
+QUAD = QUAD_TILES * P
 CHUNK = CHUNK_TILES * P
 N_CHUNKS = TOKENS // CHUNK
+N_QUADS = TOKENS // QUAD
 N_PAIRS = TOKENS // PAIR
 PAIRS_PER_CHUNK = CHUNK_TILES // PAIR_TILES
 PAIRS_PER_QUAD = QUAD_TILES // PAIR_TILES
+QUADS_PER_CHUNK = CHUNK_TILES // QUAD_TILES
 BN_STATS = 6
 BN_AGGR = 2
+
+GATE_LOW_LEAD = 2
+MULTIPLY_LAG = 1
+QUANTISE_LAG = 2
+PROJECT_LAG = 4
+STATS_LAG = 5
+SHIFT_LAG = 7
+NORMALISE_LAG = 8
 
 FLOPS = 2 * TOKENS * G * E + 2 * TOKENS * E * EO
 
@@ -40,9 +51,12 @@ def tile_tnlattention_pb_t_kernel(tc, attn, gate_low, Wg2, Wo, ln_w, ln_b, out):
     gate_low_rows = gate_low.flatten_outer_dims()
     out_rows = out.flatten_outer_dims()
 
+    def chunk_view(rows, c):
+        return rows[c * CHUNK : (c + 1) * CHUNK, :].rearrange("(p j) w -> p j w", j=CHUNK_TILES)
+
     with ExitStack() as ctx:
         consts = ctx.enter_context(tc.tile_pool(name="consts", bufs=1))
-        attn_pool = ctx.enter_context(tc.tile_pool(name="attn", bufs=N_CHUNKS))
+        attn_pool = ctx.enter_context(tc.tile_pool(name="attn", bufs=N_QUADS))
         gate_low_pool = ctx.enter_context(tc.tile_pool(name="gate_low", bufs=N_CHUNKS))
         gate_low_t_pool = ctx.enter_context(tc.tile_pool(name="gate_low_t", bufs=2))
         gate_pool = ctx.enter_context(tc.tile_pool(name="gate", bufs=3))
@@ -50,43 +64,33 @@ def tile_tnlattention_pb_t_kernel(tc, attn, gate_low, Wg2, Wo, ln_w, ln_b, out):
         mx_pool = ctx.enter_context(tc.tile_pool(name="mx", bufs=3))
         stat_pool = ctx.enter_context(tc.tile_pool(name="stat", bufs=4))
         result_pool = ctx.enter_context(tc.tile_pool(name="result", bufs=6))
-        gate_low_t_psum = ctx.enter_context(tc.psum_pool(name="gate_low_t_ps", bufs=1))
+        for_scalar_psum = ctx.enter_context(tc.psum_pool(name="for_scalar_ps", bufs=3))
         attn_t_psum = ctx.enter_context(tc.psum_pool(name="attn_t_ps", bufs=2))
-        z_psum = ctx.enter_context(tc.psum_pool(name="z_ps", bufs=3))
-        y_psum = ctx.enter_context(tc.psum_pool(name="y_ps", bufs=2))
-
-        attn_chunks = []
-        gate_low_chunks = []
-
-        def load_chunk(c):
-            rows = slice(c * CHUNK, (c + 1) * CHUNK)
-            gate_low_sb = gate_low_pool.tile([P, CHUNK_TILES, G], BF16)
-            nc.sync.dma_start(
-                out=gate_low_sb[:],
-                in_=gate_low_rows[rows, :].rearrange("(p j) g -> p j g", j=CHUNK_TILES),
-            )
-            gate_low_chunks.append(gate_low_sb)
-            attn_sb = attn_pool.tile([P, CHUNK_TILES, E], BF16)
-            nc.sync.dma_start(
-                out=attn_sb[:],
-                in_=attn_rows[rows, :].rearrange("(p j) k -> p j k", j=CHUNK_TILES),
-            )
-            attn_chunks.append(attn_sb)
+        y_psum = ctx.enter_context(tc.psum_pool(name="y_ps", bufs=3))
 
         wg2_sb = consts.tile([P, E], BF16)
         nc.sync.dma_start(out=wg2_sb[:], in_=Wg2[:, :])
-        load_chunk(0)
         wo_rows = consts.tile([P, PACK, EO], BF16)
-        nc.sync.dma_start(
-            out=wo_rows[:].rearrange("q (u e) o -> q u (e o)", e=2),
-            in_=Wo.rearrange("(u q e) o -> q u (e o)", u=2, e=2),
-        )
         ln_w_all = consts.tile([P, EO], BF16)
-        nc.sync.dma_start(out=ln_w_all[:], in_=ln_w.partition_broadcast(P))
         ln_b_all = consts.tile([P, EO], BF16)
-        nc.sync.dma_start(out=ln_b_all[:], in_=ln_b.partition_broadcast(P))
-        for c in range(1, N_CHUNKS):
-            load_chunk(c)
+        attn_quads = []
+        gate_low_chunks = []
+        for c in range(N_CHUNKS):
+            gate_low_sb = gate_low_pool.tile([P, CHUNK_TILES, G], BF16)
+            nc.sync.dma_start(out=gate_low_sb[:], in_=chunk_view(gate_low_rows, c))
+            gate_low_chunks.append(gate_low_sb)
+            for half in range(QUADS_PER_CHUNK):
+                tiles = slice(half * QUAD_TILES, (half + 1) * QUAD_TILES)
+                attn_sb = attn_pool.tile([P, QUAD_TILES, E], BF16)
+                nc.sync.dma_start(out=attn_sb[:], in_=chunk_view(attn_rows, c)[:, tiles, :])
+                attn_quads.append(attn_sb)
+            if c == 0:
+                nc.sync.dma_start(
+                    out=wo_rows[:].rearrange("q (u e) o -> q u (e o)", e=2),
+                    in_=Wo.rearrange("(u q e) o -> q u (e o)", u=2, e=2),
+                )
+                nc.sync.dma_start(out=ln_w_all[:], in_=ln_w.partition_broadcast(P))
+                nc.sync.dma_start(out=ln_b_all[:], in_=ln_b.partition_broadcast(P))
 
         ident_bf16 = consts.tile([P, P], BF16)
         make_identity(nc, ident_bf16[:])
@@ -104,43 +108,49 @@ def tile_tnlattention_pb_t_kernel(tc, attn, gate_low, Wg2, Wo, ln_w, ln_b, out):
             in_=wg2_sb[:].rearrange("g (u q e) -> g u e q", u=2, e=2),
         )
 
-        wo_grouped = consts.tile([P, EO, PACK], BF16, align_bytes=64)
-        nc.vector.tensor_copy(out=wo_grouped[:], in_=wo_rows[:].rearrange("q t o -> q o t"))
         wo_codes = consts.tile([P, EO], U32, align_bytes=64)
         wo_scales = consts.tile([P, EO], U8, align_bytes=64)
-        nc.vector.quantize_mx(
-            out=wo_codes[:].bitcast(FP8X4),
-            scales=wo_scales[:],
-            in_=wo_grouped[:].rearrange("q o t -> q (o t)"),
-        )
+
+        def quantise_wo():
+            wo_grouped = consts.tile([P, EO, PACK], BF16, align_bytes=64)
+            nc.vector.tensor_copy(out=wo_grouped[:], in_=wo_rows[:].rearrange("q t o -> q o t"))
+            nc.vector.quantize_mx(
+                out=wo_codes[:].bitcast(FP8X4),
+                scales=wo_scales[:],
+                in_=wo_grouped[:].rearrange("q o t -> q (o t)"),
+            )
+
+        gate_low_t = {}
+        gate = {}
+        attn_t = {}
+        h = {}
+        h_codes = {}
+        h_scales = {}
+        y = {}
+        mean_var = {}
+        rstd = {}
+        shift = {}
 
         def transpose_gate_low(c):
-            gate_low_t_ps = gate_low_t_psum.tile([P, CHUNK], BF16)
+            gate_low_t_ps = for_scalar_psum.tile([P, CHUNK], BF16, tag="for_scalar")
             for j in range(CHUNK_TILES):
                 nc.tensor.transpose(
                     gate_low_t_ps[:, j * P : (j + 1) * P], gate_low_chunks[c][:, j, :], ident_bf16[:]
                 )
-            gate_low_t = gate_low_t_pool.tile([P, CHUNK], BF16)
-            nc.scalar.copy(out=gate_low_t[:], in_=gate_low_t_ps[:])
-            return gate_low_t
+            gate_low_t_sb = gate_low_t_pool.tile([P, CHUNK], BF16)
+            nc.scalar.copy(out=gate_low_t_sb[:], in_=gate_low_t_ps[:])
+            gate_low_t[c] = gate_low_t_sb
 
-        def gated_product(s, gate_low_t):
+        def compute_gate(s):
             c = s // PAIRS_PER_CHUNK
             first_tile = (s % PAIRS_PER_CHUNK) * PAIR_TILES
-            attn_t_ps = attn_t_psum.tile([P, 2, PAIR], F32)
-            for i in range(PAIR_TILES):
-                words = attn_chunks[c][:, first_tile + i, :].bitcast(F32)
-                for u in range(2):
-                    nc.tensor.transpose(
-                        attn_t_ps[:, u, i * P : (i + 1) * P], words[:, u * P : (u + 1) * P], ident_f32[:]
-                    )
             gate_sb = gate_pool.tile([P, PAIR, PACK], F32)
             for i in range(PAIR_TILES):
                 tokens = slice((first_tile + i) * P, (first_tile + i + 1) * P)
-                z_ps = z_psum.tile([P, PACK, P], F32)
+                z_ps = for_scalar_psum.tile([P, PACK, P], F32, tag="for_scalar")
                 for t in range(PACK):
                     nc.tensor.matmul(
-                        out=z_ps[:, t, :], lhsT=wg2_by_t[:, t, :], rhs=gate_low_t[:, tokens],
+                        out=z_ps[:, t, :], lhsT=wg2_by_t[:, t, :], rhs=gate_low_t[c][:, tokens],
                         start=True, stop=True,
                     )
                 nc.scalar.activation(
@@ -148,55 +158,86 @@ def tile_tnlattention_pb_t_kernel(tc, attn, gate_low, Wg2, Wo, ln_w, ln_b, out):
                     in_=z_ps[:].rearrange("q t n -> q n t"),
                     func=ACT.Sigmoid,
                 )
+            gate[s] = gate_sb
+
+        def transpose_attn(s):
+            first_tile = (s % PAIRS_PER_QUAD) * PAIR_TILES
+            attn_t_ps = attn_t_psum.tile([P, 2, PAIR], F32)
+            for i in range(PAIR_TILES):
+                words = attn_quads[s // PAIRS_PER_QUAD][:, first_tile + i, :].bitcast(F32)
+                for u in range(2):
+                    nc.tensor.transpose(
+                        attn_t_ps[:, u, i * P : (i + 1) * P], words[:, u * P : (u + 1) * P], ident_f32[:]
+                    )
+            attn_t[s] = attn_t_ps
+
+        def multiply(s):
             h_sb = h_pool.tile([P, PAIR, PACK], BF16, align_bytes=64)
             nc.vector.tensor_tensor(
                 out=h_sb[:].rearrange("q n (u e) -> q n u e", e=2),
-                in0=attn_t_ps[:].bitcast(BF16).rearrange("q u (n e) -> q n u e", e=2),
-                in1=gate_sb[:].rearrange("q n (u e) -> q n u e", e=2),
+                in0=attn_t[s][:].bitcast(BF16).rearrange("q u (n e) -> q n u e", e=2),
+                in1=gate[s][:].rearrange("q n (u e) -> q n u e", e=2),
                 op=ALU.mult,
             )
-            return h_sb
+            h[s] = h_sb
 
-        def project(h_sb, y_ps, first_slot):
-            h_codes = mx_pool.tile([P, PAIR], U32, align_bytes=64)
-            h_scales = mx_pool.tile([P, PAIR], U8, align_bytes=64)
+        def quantise(s):
+            quad = s // PAIRS_PER_QUAD
+            if s % PAIRS_PER_QUAD == 0:
+                codes = mx_pool.tile([P, QUAD], U32, align_bytes=64)
+                scales = mx_pool.tile([P, QUAD], U8, align_bytes=64)
+                h_codes[quad] = codes
+                h_scales[quad] = scales
+            tokens = slice((s % PAIRS_PER_QUAD) * PAIR, (s % PAIRS_PER_QUAD + 1) * PAIR)
             nc.vector.quantize_mx(
-                out=h_codes[:].bitcast(FP8X4),
-                scales=h_scales[:],
-                in_=h_sb[:].rearrange("q n t -> q (n t)"),
+                out=h_codes[quad][:, tokens].bitcast(FP8X4),
+                scales=h_scales[quad][:, tokens],
+                in_=h[s][:].rearrange("q n t -> q (n t)"),
             )
-            for i in range(PAIR_TILES):
+
+        def project(quad):
+            y_ps = y_psum.tile([P, QUAD_TILES, EO], F32)
+            for i in range(QUAD_TILES):
                 tokens = slice(i * P, (i + 1) * P)
                 nc.tensor.matmul_mx(
-                    out=y_ps[:, first_slot + i, :],
-                    lhsT=h_codes[:, tokens].bitcast(FP8X4),
-                    lhsT_scale=h_scales[:, tokens],
+                    out=y_ps[:, i, :],
+                    lhsT=h_codes[quad][:, tokens].bitcast(FP8X4),
+                    lhsT_scale=h_scales[quad][:, tokens],
                     rhs=wo_codes[:].bitcast(FP8X4),
                     rhs_scale=wo_scales[:],
                     start=True,
                     stop=True,
                 )
+            y[quad] = y_ps
 
-        def layer_norm_and_store(quad, y_ps):
+        def statistics(quad):
             stats = stat_pool.tile([P, QUAD_TILES, BN_STATS], F32)
-            mean_var = stat_pool.tile([P, QUAD_TILES, BN_AGGR], F32)
+            mean_var_sb = stat_pool.tile([P, QUAD_TILES, BN_AGGR], F32)
             for i in range(QUAD_TILES):
-                nc.vector.bn_stats(out=stats[:, i, :], in_=y_ps[:, i, :])
+                nc.vector.bn_stats(out=stats[:, i, :], in_=y[quad][:, i, :])
             for i in range(QUAD_TILES):
-                nc.vector.bn_aggr(out=mean_var[:, i, :], in_=stats[:, i, :])
+                nc.vector.bn_aggr(out=mean_var_sb[:, i, :], in_=stats[:, i, :])
             var_eps = stat_pool.tile([P, QUAD_TILES], F32)
-            nc.vector.tensor_scalar_add(out=var_eps[:], in0=mean_var[:, :, 1], scalar1=LN_EPS)
-            rstd = stat_pool.tile([P, QUAD_TILES], F32)
-            nc.gpsimd.tensor_tensor(out=rstd[:], in0=var_eps[:], in1=minus_half[:], op=ALU.pow)
-            shift = stat_pool.tile([P, QUAD_TILES], F32)
+            nc.vector.tensor_scalar_add(out=var_eps[:], in0=mean_var_sb[:, :, 1], scalar1=LN_EPS)
+            rstd_sb = stat_pool.tile([P, QUAD_TILES], F32)
+            nc.gpsimd.tensor_tensor(out=rstd_sb[:], in0=var_eps[:], in1=minus_half[:], op=ALU.pow)
+            mean_var[quad] = mean_var_sb
+            rstd[quad] = rstd_sb
+
+        def compute_shift(quad):
+            shift_sb = stat_pool.tile([P, QUAD_TILES], F32)
             nc.vector.scalar_tensor_tensor(
-                out=shift[:], in0=mean_var[:, :, 0], scalar=-1.0, in1=rstd[:], op0=ALU.mult, op1=ALU.mult
+                out=shift_sb[:], in0=mean_var[quad][:, :, 0], scalar=-1.0, in1=rstd[quad][:],
+                op0=ALU.mult, op1=ALU.mult,
             )
+            shift[quad] = shift_sb
+
+        def normalise_and_store(quad):
             result = result_pool.tile([P, QUAD_TILES, EO], F32)
             for i in range(QUAD_TILES):
                 nc.scalar.activation(
-                    out=result[:, i, :], in_=y_ps[:, i, :], func=ACT.Identity,
-                    bias=shift[:, i : i + 1], scale=rstd[:, i : i + 1],
+                    out=result[:, i, :], in_=y[quad][:, i, :], func=ACT.Identity,
+                    bias=shift[quad][:, i : i + 1], scale=rstd[quad][:, i : i + 1],
                 )
             whole = [P, QUAD_TILES, EO]
             nc.gpsimd.tensor_tensor(
@@ -205,24 +246,47 @@ def tile_tnlattention_pb_t_kernel(tc, attn, gate_low, Wg2, Wo, ln_w, ln_b, out):
             nc.gpsimd.tensor_tensor(
                 out=result[:], in0=result[:], in1=ln_b_all[:].unsqueeze(1).to_broadcast(whole), op=ALU.add
             )
-            c = quad * QUAD_TILES // CHUNK_TILES
-            first_tile = quad * QUAD_TILES % CHUNK_TILES
-            chunk_rows = out_rows[c * CHUNK : (c + 1) * CHUNK, :].rearrange("(p j) o -> p j o", j=CHUNK_TILES)
-            nc.sync.dma_start(out=chunk_rows[:, first_tile : first_tile + QUAD_TILES, :], in_=result[:])
+            first_tile = (quad % QUADS_PER_CHUNK) * QUAD_TILES
+            nc.sync.dma_start(
+                out=chunk_view(out_rows, quad // QUADS_PER_CHUNK)[:, first_tile : first_tile + QUAD_TILES, :],
+                in_=result[:],
+            )
 
-        h_tiles = []
-        gate_low_t = None
-        y_ps = None
-        for s in range(N_PAIRS + 1):
-            if s < N_PAIRS:
-                if s % PAIRS_PER_CHUNK == 0:
-                    gate_low_t = transpose_gate_low(s // PAIRS_PER_CHUNK)
-                h_tiles.append(gated_product(s, gate_low_t))
-            if s >= 1:
-                done = s - 1
-                slot = done % PAIRS_PER_QUAD
-                if slot == 0:
-                    y_ps = y_psum.tile([P, QUAD_TILES, EO], F32)
-                project(h_tiles[done], y_ps, slot * PAIR_TILES)
-                if slot == PAIRS_PER_QUAD - 1:
-                    layer_norm_and_store(done // PAIRS_PER_QUAD, y_ps)
+        def pair_due(step, lag):
+            s = step - lag
+            return s if 0 <= s < N_PAIRS else None
+
+        def quad_due(step, lag):
+            quad, rest = divmod(step - lag, PAIRS_PER_QUAD)
+            return quad if rest == 0 and 0 <= quad < N_QUADS else None
+
+        with tc.manual_schedule():
+            transpose_gate_low(0)
+            for step in range(N_PAIRS + NORMALISE_LAG):
+                s = pair_due(step, 0)
+                if s is not None:
+                    compute_gate(s)
+                    transpose_attn(s)
+                ahead = pair_due(step, -GATE_LOW_LEAD)
+                if ahead is not None and ahead % PAIRS_PER_CHUNK == 0:
+                    transpose_gate_low(ahead // PAIRS_PER_CHUNK)
+                quad = quad_due(step, PROJECT_LAG)
+                if quad is not None:
+                    project(quad)
+                quad = quad_due(step, SHIFT_LAG)
+                if quad is not None:
+                    compute_shift(quad)
+                s = pair_due(step, MULTIPLY_LAG)
+                if s is not None:
+                    multiply(s)
+                if step == QUANTISE_LAG:
+                    quantise_wo()
+                s = pair_due(step, QUANTISE_LAG)
+                if s is not None:
+                    quantise(s)
+                quad = quad_due(step, STATS_LAG)
+                if quad is not None:
+                    statistics(quad)
+                quad = quad_due(step, NORMALISE_LAG)
+                if quad is not None:
+                    normalise_and_store(quad)

@@ -36,11 +36,12 @@ BN_AGGR = 2
 
 GATE_LOW_LEAD = 2
 MULTIPLY_LAG = 1
-QUANTISE_LAG = 2
+QUANTISE_LAG = 3
 PROJECT_LAG = 4
 STATS_LAG = 5
-SHIFT_LAG = 7
+RSTD_LAG = 6
 NORMALISE_LAG = 8
+VECTOR_EVERY = 4
 
 FLOPS = 2 * TOKENS * G * E + 2 * TOKENS * E * EO
 
@@ -131,6 +132,9 @@ def tile_tnlattention_pb_t_kernel(tc, attn, gate_low, Wg2, Wo, ln_w, ln_b, out):
         rstd = {}
         shift = {}
 
+        def by_vector(quad):
+            return quad % VECTOR_EVERY == VECTOR_EVERY - 1
+
         def transpose_gate_low(c):
             gate_low_t_ps = for_scalar_psum.tile([P, CHUNK], BF16, tag="for_scalar")
             for j in range(CHUNK_TILES):
@@ -172,28 +176,28 @@ def tile_tnlattention_pb_t_kernel(tc, attn, gate_low, Wg2, Wo, ln_w, ln_b, out):
             attn_t[s] = attn_t_ps
 
         def multiply(s):
-            h_sb = h_pool.tile([P, PAIR, PACK], BF16, align_bytes=64)
+            quad = s // PAIRS_PER_QUAD
+            if s % PAIRS_PER_QUAD == 0:
+                h_sb = h_pool.tile([P, QUAD, PACK], BF16, align_bytes=64)
+                h[quad] = h_sb
+            tokens = slice((s % PAIRS_PER_QUAD) * PAIR, (s % PAIRS_PER_QUAD + 1) * PAIR)
             nc.vector.tensor_tensor(
-                out=h_sb[:].rearrange("q n (u e) -> q n u e", e=2),
+                out=h[quad][:, tokens, :].rearrange("q n (u e) -> q n u e", e=2),
                 in0=attn_t[s][:].bitcast(BF16).rearrange("q u (n e) -> q n u e", e=2),
                 in1=gate[s][:].rearrange("q n (u e) -> q n u e", e=2),
                 op=ALU.mult,
             )
-            h[s] = h_sb
 
-        def quantise(s):
-            quad = s // PAIRS_PER_QUAD
-            if s % PAIRS_PER_QUAD == 0:
-                codes = mx_pool.tile([P, QUAD], U32, align_bytes=64)
-                scales = mx_pool.tile([P, QUAD], U8, align_bytes=64)
-                h_codes[quad] = codes
-                h_scales[quad] = scales
-            tokens = slice((s % PAIRS_PER_QUAD) * PAIR, (s % PAIRS_PER_QUAD + 1) * PAIR)
+        def quantise(quad):
+            codes = mx_pool.tile([P, QUAD], U32, align_bytes=64)
+            scales = mx_pool.tile([P, QUAD], U8, align_bytes=64)
             nc.vector.quantize_mx(
-                out=h_codes[quad][:, tokens].bitcast(FP8X4),
-                scales=h_scales[quad][:, tokens],
-                in_=h[s][:].rearrange("q n t -> q (n t)"),
+                out=codes[:].bitcast(FP8X4),
+                scales=scales[:],
+                in_=h[quad][:].rearrange("q n t -> q (n t)"),
             )
+            h_codes[quad] = codes
+            h_scales[quad] = scales
 
         def project(quad):
             y_ps = y_psum.tile([P, QUAD_TILES, EO], F32)
@@ -217,35 +221,50 @@ def tile_tnlattention_pb_t_kernel(tc, attn, gate_low, Wg2, Wo, ln_w, ln_b, out):
                 nc.vector.bn_stats(out=stats[:, i, :], in_=y[quad][:, i, :])
             for i in range(QUAD_TILES):
                 nc.vector.bn_aggr(out=mean_var_sb[:, i, :], in_=stats[:, i, :])
+            mean_var[quad] = mean_var_sb
+
+        def compute_rstd(quad):
             var_eps = stat_pool.tile([P, QUAD_TILES], F32)
-            nc.vector.tensor_scalar_add(out=var_eps[:], in0=mean_var_sb[:, :, 1], scalar1=LN_EPS)
+            nc.scalar.activation(
+                out=var_eps[:], in_=mean_var[quad][:, :, 1], func=ACT.Identity, bias=LN_EPS, scale=1.0
+            )
             rstd_sb = stat_pool.tile([P, QUAD_TILES], F32)
             nc.gpsimd.tensor_tensor(out=rstd_sb[:], in0=var_eps[:], in1=minus_half[:], op=ALU.pow)
-            mean_var[quad] = mean_var_sb
             rstd[quad] = rstd_sb
-
-        def compute_shift(quad):
-            shift_sb = stat_pool.tile([P, QUAD_TILES], F32)
-            nc.vector.scalar_tensor_tensor(
-                out=shift_sb[:], in0=mean_var[quad][:, :, 0], scalar=-1.0, in1=rstd[quad][:],
-                op0=ALU.mult, op1=ALU.mult,
-            )
-            shift[quad] = shift_sb
+            if not by_vector(quad):
+                neg_mean = stat_pool.tile([P, QUAD_TILES], F32)
+                nc.scalar.mul(out=neg_mean[:], in_=mean_var[quad][:, :, 0], mul=-1.0)
+                shift_sb = stat_pool.tile([P, QUAD_TILES], F32)
+                nc.gpsimd.tensor_tensor(out=shift_sb[:], in0=neg_mean[:], in1=rstd_sb[:], op=ALU.mult)
+                shift[quad] = shift_sb
 
         def normalise_and_store(quad):
             result = result_pool.tile([P, QUAD_TILES, EO], F32)
-            for i in range(QUAD_TILES):
-                nc.scalar.activation(
-                    out=result[:, i, :], in_=y[quad][:, i, :], func=ACT.Identity,
-                    bias=shift[quad][:, i : i + 1], scale=rstd[quad][:, i : i + 1],
+            if by_vector(quad):
+                centred = result_pool.tile([P, QUAD_TILES, EO], F32)
+                for i in range(QUAD_TILES):
+                    nc.vector.scalar_tensor_tensor(
+                        out=centred[:, i, :], in0=y[quad][:, i, :], scalar=mean_var[quad][:, i, 0:1],
+                        in1=ln_w_all[:], op0=ALU.subtract, op1=ALU.mult,
+                    )
+                for i in range(QUAD_TILES):
+                    nc.vector.scalar_tensor_tensor(
+                        out=result[:, i, :], in0=centred[:, i, :], scalar=rstd[quad][:, i : i + 1],
+                        in1=ln_b_all[:], op0=ALU.mult, op1=ALU.add,
+                    )
+            else:
+                for i in range(QUAD_TILES):
+                    nc.scalar.activation(
+                        out=result[:, i, :], in_=y[quad][:, i, :], func=ACT.Identity,
+                        bias=shift[quad][:, i : i + 1], scale=rstd[quad][:, i : i + 1],
+                    )
+                whole = [P, QUAD_TILES, EO]
+                nc.gpsimd.tensor_tensor(
+                    out=result[:], in0=result[:], in1=ln_w_all[:].unsqueeze(1).to_broadcast(whole), op=ALU.mult
                 )
-            whole = [P, QUAD_TILES, EO]
-            nc.gpsimd.tensor_tensor(
-                out=result[:], in0=result[:], in1=ln_w_all[:].unsqueeze(1).to_broadcast(whole), op=ALU.mult
-            )
-            nc.gpsimd.tensor_tensor(
-                out=result[:], in0=result[:], in1=ln_b_all[:].unsqueeze(1).to_broadcast(whole), op=ALU.add
-            )
+                nc.gpsimd.tensor_tensor(
+                    out=result[:], in0=result[:], in1=ln_b_all[:].unsqueeze(1).to_broadcast(whole), op=ALU.add
+                )
             first_tile = (quad % QUADS_PER_CHUNK) * QUAD_TILES
             nc.sync.dma_start(
                 out=chunk_view(out_rows, quad // QUADS_PER_CHUNK)[:, first_tile : first_tile + QUAD_TILES, :],
@@ -273,17 +292,17 @@ def tile_tnlattention_pb_t_kernel(tc, attn, gate_low, Wg2, Wo, ln_w, ln_b, out):
                 quad = quad_due(step, PROJECT_LAG)
                 if quad is not None:
                     project(quad)
-                quad = quad_due(step, SHIFT_LAG)
+                quad = quad_due(step, RSTD_LAG)
                 if quad is not None:
-                    compute_shift(quad)
+                    compute_rstd(quad)
                 s = pair_due(step, MULTIPLY_LAG)
                 if s is not None:
                     multiply(s)
                 if step == QUANTISE_LAG:
                     quantise_wo()
-                s = pair_due(step, QUANTISE_LAG)
-                if s is not None:
-                    quantise(s)
+                quad = quad_due(step, QUANTISE_LAG)
+                if quad is not None:
+                    quantise(quad)
                 quad = quad_due(step, STATS_LAG)
                 if quad is not None:
                     statistics(quad)

@@ -72,8 +72,8 @@ def tile_tnlattention_pb_t_kernel(tc, attn, gate_low, Wg2, Wo, ln_w, ln_b, out):
         wg2_sb = consts.tile([P, E], BF16)
         nc.sync.dma_start(out=wg2_sb[:], in_=Wg2[:, :])
         wo_rows = consts.tile([P, PACK, EO], BF16)
-        ln_w_all = consts.tile([P, EO], BF16)
-        ln_b_all = consts.tile([P, EO], BF16)
+        ln_w_bf16 = consts.tile([P, EO], BF16)
+        ln_b_bf16 = consts.tile([P, EO], BF16)
         attn_quads = []
         gate_low_chunks = []
         for c in range(N_CHUNKS):
@@ -90,8 +90,8 @@ def tile_tnlattention_pb_t_kernel(tc, attn, gate_low, Wg2, Wo, ln_w, ln_b, out):
                     out=wo_rows[:].rearrange("q (u e) o -> q u (e o)", e=2),
                     in_=Wo.rearrange("(u q e) o -> q u (e o)", u=2, e=2),
                 )
-                nc.sync.dma_start(out=ln_w_all[:], in_=ln_w.partition_broadcast(P))
-                nc.sync.dma_start(out=ln_b_all[:], in_=ln_b.partition_broadcast(P))
+                nc.sync.dma_start(out=ln_w_bf16[:], in_=ln_w.partition_broadcast(P))
+                nc.sync.dma_start(out=ln_b_bf16[:], in_=ln_b.partition_broadcast(P))
 
         ident_bf16 = consts.tile([P, P], BF16)
         make_identity(nc, ident_bf16[:])
@@ -111,6 +111,13 @@ def tile_tnlattention_pb_t_kernel(tc, attn, gate_low, Wg2, Wo, ln_w, ln_b, out):
 
         wo_codes = consts.tile([P, EO], U32, align_bytes=64)
         wo_scales = consts.tile([P, EO], U8, align_bytes=64)
+        ln_w_quad = consts.tile([P, QUAD_TILES, EO], F32)
+        ln_b_quad = consts.tile([P, QUAD_TILES, EO], F32)
+
+        def spread_ln_w_and_b():
+            whole = [P, QUAD_TILES, EO]
+            nc.vector.tensor_copy(out=ln_w_quad[:], in_=ln_w_bf16[:].unsqueeze(1).to_broadcast(whole))
+            nc.vector.tensor_copy(out=ln_b_quad[:], in_=ln_b_bf16[:].unsqueeze(1).to_broadcast(whole))
 
         def quantise_wo():
             wo_grouped = consts.tile([P, EO, PACK], BF16, align_bytes=64)
@@ -245,12 +252,12 @@ def tile_tnlattention_pb_t_kernel(tc, attn, gate_low, Wg2, Wo, ln_w, ln_b, out):
                 for i in range(QUAD_TILES):
                     nc.vector.scalar_tensor_tensor(
                         out=centred[:, i, :], in0=y[quad][:, i, :], scalar=mean_var[quad][:, i, 0:1],
-                        in1=ln_w_all[:], op0=ALU.subtract, op1=ALU.mult,
+                        in1=ln_w_quad[:, i, :], op0=ALU.subtract, op1=ALU.mult,
                     )
                 for i in range(QUAD_TILES):
                     nc.vector.scalar_tensor_tensor(
                         out=result[:, i, :], in0=centred[:, i, :], scalar=rstd[quad][:, i : i + 1],
-                        in1=ln_b_all[:], op0=ALU.mult, op1=ALU.add,
+                        in1=ln_b_quad[:, i, :], op0=ALU.mult, op1=ALU.add,
                     )
             else:
                 for i in range(QUAD_TILES):
@@ -258,13 +265,8 @@ def tile_tnlattention_pb_t_kernel(tc, attn, gate_low, Wg2, Wo, ln_w, ln_b, out):
                         out=result[:, i, :], in_=y[quad][:, i, :], func=ACT.Identity,
                         bias=shift[quad][:, i : i + 1], scale=rstd[quad][:, i : i + 1],
                     )
-                whole = [P, QUAD_TILES, EO]
-                nc.gpsimd.tensor_tensor(
-                    out=result[:], in0=result[:], in1=ln_w_all[:].unsqueeze(1).to_broadcast(whole), op=ALU.mult
-                )
-                nc.gpsimd.tensor_tensor(
-                    out=result[:], in0=result[:], in1=ln_b_all[:].unsqueeze(1).to_broadcast(whole), op=ALU.add
-                )
+                nc.gpsimd.tensor_tensor(out=result[:], in0=result[:], in1=ln_w_quad[:], op=ALU.mult)
+                nc.gpsimd.tensor_tensor(out=result[:], in0=result[:], in1=ln_b_quad[:], op=ALU.add)
             first_tile = (quad % QUADS_PER_CHUNK) * QUAD_TILES
             nc.sync.dma_start(
                 out=chunk_view(out_rows, quad // QUADS_PER_CHUNK)[:, first_tile : first_tile + QUAD_TILES, :],
@@ -300,6 +302,7 @@ def tile_tnlattention_pb_t_kernel(tc, attn, gate_low, Wg2, Wo, ln_w, ln_b, out):
                     multiply(s)
                 if step == QUANTISE_LAG:
                     quantise_wo()
+                    spread_ln_w_and_b()
                 quad = quad_due(step, QUANTISE_LAG)
                 if quad is not None:
                     quantise(quad)

@@ -41,7 +41,7 @@ PROJECT_LAG = 4
 STATS_LAG = 5
 RSTD_LAG = 6
 NORMALISE_LAG = 8
-VECTOR_EVERY = 4
+SCALE_LAG = 10
 
 FLOPS = 2 * TOKENS * G * E + 2 * TOKENS * E * EO
 
@@ -139,8 +139,10 @@ def tile_tnlattention_pb_t_kernel(tc, attn, gate_low, Wg2, Wo, ln_w, ln_b, out):
         rstd = {}
         shift = {}
 
+        normalised = {}
+
         def by_vector(quad):
-            return quad % VECTOR_EVERY == VECTOR_EVERY - 1
+            return quad == N_QUADS - 1
 
         def transpose_gate_low(c):
             gate_low_t_ps = for_scalar_psum.tile([P, CHUNK], BF16, tag="for_scalar")
@@ -245,33 +247,42 @@ def tile_tnlattention_pb_t_kernel(tc, attn, gate_low, Wg2, Wo, ln_w, ln_b, out):
                 nc.gpsimd.tensor_tensor(out=shift_sb[:], in0=neg_mean[:], in1=rstd_sb[:], op=ALU.mult)
                 shift[quad] = shift_sb
 
-        def normalise_and_store(quad):
-            result = result_pool.tile([P, QUAD_TILES, EO], F32)
-            if by_vector(quad):
-                centred = result_pool.tile([P, QUAD_TILES, EO], F32)
-                for i in range(QUAD_TILES):
-                    nc.vector.scalar_tensor_tensor(
-                        out=centred[:, i, :], in0=y[quad][:, i, :], scalar=mean_var[quad][:, i, 0:1],
-                        in1=ln_w_quad[:, i, :], op0=ALU.subtract, op1=ALU.mult,
-                    )
-                for i in range(QUAD_TILES):
-                    nc.vector.scalar_tensor_tensor(
-                        out=result[:, i, :], in0=centred[:, i, :], scalar=rstd[quad][:, i : i + 1],
-                        in1=ln_b_quad[:, i, :], op0=ALU.mult, op1=ALU.add,
-                    )
-            else:
-                for i in range(QUAD_TILES):
-                    nc.scalar.activation(
-                        out=result[:, i, :], in_=y[quad][:, i, :], func=ACT.Identity,
-                        bias=shift[quad][:, i : i + 1], scale=rstd[quad][:, i : i + 1],
-                    )
-                nc.gpsimd.tensor_tensor(out=result[:], in0=result[:], in1=ln_w_quad[:], op=ALU.mult)
-                nc.gpsimd.tensor_tensor(out=result[:], in0=result[:], in1=ln_b_quad[:], op=ALU.add)
+        def store(quad, result):
             first_tile = (quad % QUADS_PER_CHUNK) * QUAD_TILES
             nc.sync.dma_start(
                 out=chunk_view(out_rows, quad // QUADS_PER_CHUNK)[:, first_tile : first_tile + QUAD_TILES, :],
                 in_=result[:],
             )
+
+        def normalise(quad):
+            normalised_sb = result_pool.tile([P, QUAD_TILES, EO], F32)
+            for i in range(QUAD_TILES):
+                nc.scalar.activation(
+                    out=normalised_sb[:, i, :], in_=y[quad][:, i, :], func=ACT.Identity,
+                    bias=shift[quad][:, i : i + 1], scale=rstd[quad][:, i : i + 1],
+                )
+            normalised[quad] = normalised_sb
+
+        def scale_and_store(quad):
+            result = result_pool.tile([P, QUAD_TILES, EO], F32)
+            nc.vector.tensor_tensor(out=result[:], in0=normalised[quad][:], in1=ln_w_quad[:], op=ALU.mult)
+            nc.gpsimd.tensor_tensor(out=result[:], in0=result[:], in1=ln_b_quad[:], op=ALU.add)
+            store(quad, result)
+
+        def finish_on_vector(quad):
+            centred = result_pool.tile([P, QUAD_TILES, EO], F32)
+            result = result_pool.tile([P, QUAD_TILES, EO], F32)
+            for i in range(QUAD_TILES):
+                nc.vector.scalar_tensor_tensor(
+                    out=centred[:, i, :], in0=y[quad][:, i, :], scalar=mean_var[quad][:, i, 0:1],
+                    in1=ln_w_quad[:, i, :], op0=ALU.subtract, op1=ALU.mult,
+                )
+            for i in range(QUAD_TILES):
+                nc.vector.scalar_tensor_tensor(
+                    out=result[:, i, :], in0=centred[:, i, :], scalar=rstd[quad][:, i : i + 1],
+                    in1=ln_b_quad[:, i, :], op0=ALU.mult, op1=ALU.add,
+                )
+            store(quad, result)
 
         def pair_due(step, lag):
             s = step - lag
@@ -283,7 +294,7 @@ def tile_tnlattention_pb_t_kernel(tc, attn, gate_low, Wg2, Wo, ln_w, ln_b, out):
 
         with tc.manual_schedule():
             transpose_gate_low(0)
-            for step in range(N_PAIRS + NORMALISE_LAG):
+            for step in range(N_PAIRS + SCALE_LAG):
                 s = pair_due(step, 0)
                 if s is not None:
                     compute_gate(s)
@@ -309,6 +320,12 @@ def tile_tnlattention_pb_t_kernel(tc, attn, gate_low, Wg2, Wo, ln_w, ln_b, out):
                 quad = quad_due(step, STATS_LAG)
                 if quad is not None:
                     statistics(quad)
+                quad = quad_due(step, SCALE_LAG)
+                if quad is not None and not by_vector(quad):
+                    scale_and_store(quad)
                 quad = quad_due(step, NORMALISE_LAG)
                 if quad is not None:
-                    normalise_and_store(quad)
+                    if by_vector(quad):
+                        finish_on_vector(quad)
+                    else:
+                        normalise(quad)

from contextlib import ExitStack

import concourse.mybir as mybir
from concourse.masks import make_identity

F32 = mybir.dt.float32
BF16 = mybir.dt.bfloat16
U32 = mybir.dt.uint32
U8 = mybir.dt.uint8
FP8X4 = mybir.dt.float8_e4m3fn_x4
ACT = mybir.ActivationFunctionType
ALU = mybir.AluOpType

P = 128
PACK = 4
TOKENS = 4 * 2048
E = 512
G = 128
EO = 128
LN_EPS = 1e-5

PAIR_TILES = 2
QUAD_TILES = 4
CHUNK_TILES = 8
PAIR = PAIR_TILES * P
QUAD = QUAD_TILES * P
CHUNK = CHUNK_TILES * P
N_CHUNKS = TOKENS // CHUNK
N_QUADS = TOKENS // QUAD
N_PAIRS = TOKENS // PAIR
PAIRS_PER_CHUNK = CHUNK_TILES // PAIR_TILES
PAIRS_PER_QUAD = QUAD_TILES // PAIR_TILES
QUADS_PER_CHUNK = CHUNK_TILES // QUAD_TILES
BN_STATS = 6
BN_AGGR = 2

GATE_LOW_LEAD = 2
MULTIPLY_LAG = 1
QUANTISE_LAG = 3
PROJECT_LAG = 4
STATS_LAG = 5
RSTD_LAG = 6
NORMALISE_LAG = 8
SCALE_LAG = 10

FLOPS = 2 * TOKENS * G * E + 2 * TOKENS * E * EO


def tile_tnlattention_pb_t_kernel(tc, attn, gate_low, Wg2, Wo, ln_w, ln_b, out):
    nc = tc.nc
    attn_rows = attn.flatten_outer_dims()
    gate_low_rows = gate_low.flatten_outer_dims()
    out_rows = out.flatten_outer_dims()

    def chunk_view(rows, c):
        return rows[c * CHUNK : (c + 1) * CHUNK, :].rearrange("(p j) w -> p j w", j=CHUNK_TILES)

    with ExitStack() as ctx:
        consts = ctx.enter_context(tc.tile_pool(name="consts", bufs=1))
        attn_pool = ctx.enter_context(tc.tile_pool(name="attn", bufs=N_QUADS))
        gate_low_pool = ctx.enter_context(tc.tile_pool(name="gate_low", bufs=N_CHUNKS))
        gate_low_t_pool = ctx.enter_context(tc.tile_pool(name="gate_low_t", bufs=2))
        gate_pool = ctx.enter_context(tc.tile_pool(name="gate", bufs=3))
        h_pool = ctx.enter_context(tc.tile_pool(name="h", bufs=3))
        mx_pool = ctx.enter_context(tc.tile_pool(name="mx", bufs=3))
        stat_pool = ctx.enter_context(tc.tile_pool(name="stat", bufs=4))
        result_pool = ctx.enter_context(tc.tile_pool(name="result", bufs=6))
        for_scalar_psum = ctx.enter_context(tc.psum_pool(name="for_scalar_ps", bufs=3))
        attn_t_psum = ctx.enter_context(tc.psum_pool(name="attn_t_ps", bufs=2))
        y_psum = ctx.enter_context(tc.psum_pool(name="y_ps", bufs=3))

        wg2_sb = consts.tile([P, E], BF16)
        nc.sync.dma_start(out=wg2_sb[:], in_=Wg2[:, :])
        wo_rows = consts.tile([P, PACK, EO], BF16)
        ln_w_bf16 = consts.tile([P, EO], BF16)
        ln_b_bf16 = consts.tile([P, EO], BF16)
        attn_quads = []
        gate_low_chunks = []
        for c in range(N_CHUNKS):
            gate_low_sb = gate_low_pool.tile([P, CHUNK_TILES, G], BF16)
            nc.sync.dma_start(out=gate_low_sb[:], in_=chunk_view(gate_low_rows, c))
            gate_low_chunks.append(gate_low_sb)
            for half in range(QUADS_PER_CHUNK):
                tiles = slice(half * QUAD_TILES, (half + 1) * QUAD_TILES)
                attn_sb = attn_pool.tile([P, QUAD_TILES, E], BF16)
                nc.sync.dma_start(out=attn_sb[:], in_=chunk_view(attn_rows, c)[:, tiles, :])
                attn_quads.append(attn_sb)
            if c == 0:
                nc.sync.dma_start(
                    out=wo_rows[:].rearrange("q (u e) o -> q u (e o)", e=2),
                    in_=Wo.rearrange("(u q e) o -> q u (e o)", u=2, e=2),
                )
                nc.sync.dma_start(out=ln_w_bf16[:], in_=ln_w.partition_broadcast(P))
                nc.sync.dma_start(out=ln_b_bf16[:], in_=ln_b.partition_broadcast(P))

        ident_bf16 = consts.tile([P, P], BF16)
        make_identity(nc, ident_bf16[:])
        ident_f32 = consts.tile([P, P], F32)
        make_identity(nc, ident_f32[:])
        minus_half = consts.tile([P, QUAD_TILES], F32)
        nc.vector.memset(minus_half[:], -0.5)
        warm = consts.tile([P, 1], F32)
        nc.vector.memset(warm[:], 0.0)
        nc.scalar.activation(out=warm[:], in_=warm[:], func=ACT.Sigmoid)

        wg2_by_t = consts.tile([P, PACK, P], BF16)
        nc.vector.tensor_copy(
            out=wg2_by_t[:].rearrange("g (u e) q -> g u e q", e=2),
            in_=wg2_sb[:].rearrange("g (u q e) -> g u e q", u=2, e=2),
        )

        wo_codes = consts.tile([P, EO], U32, align_bytes=64)
        wo_scales = consts.tile([P, EO], U8, align_bytes=64)
        ln_w_quad = consts.tile([P, QUAD_TILES, EO], F32)
        ln_b_quad = consts.tile([P, QUAD_TILES, EO], F32)

        def spread_ln_w_and_b():
            whole = [P, QUAD_TILES, EO]
            nc.vector.tensor_copy(out=ln_w_quad[:], in_=ln_w_bf16[:].unsqueeze(1).to_broadcast(whole))
            nc.vector.tensor_copy(out=ln_b_quad[:], in_=ln_b_bf16[:].unsqueeze(1).to_broadcast(whole))

        def quantise_wo():
            wo_grouped = consts.tile([P, EO, PACK], BF16, align_bytes=64)
            nc.vector.tensor_copy(out=wo_grouped[:], in_=wo_rows[:].rearrange("q t o -> q o t"))
            nc.vector.quantize_mx(
                out=wo_codes[:].bitcast(FP8X4),
                scales=wo_scales[:],
                in_=wo_grouped[:].rearrange("q o t -> q (o t)"),
            )

        gate_low_t = {}
        gate = {}
        attn_t = {}
        h = {}
        h_codes = {}
        h_scales = {}
        y = {}
        mean_var = {}
        rstd = {}
        shift = {}

        normalised = {}

        def by_vector(quad):
            return quad == N_QUADS - 1

        def transpose_gate_low(c):
            gate_low_t_ps = for_scalar_psum.tile([P, CHUNK], BF16, tag="for_scalar")
            for j in range(CHUNK_TILES):
                nc.tensor.transpose(
                    gate_low_t_ps[:, j * P : (j + 1) * P], gate_low_chunks[c][:, j, :], ident_bf16[:]
                )
            gate_low_t_sb = gate_low_t_pool.tile([P, CHUNK], BF16)
            nc.scalar.copy(out=gate_low_t_sb[:], in_=gate_low_t_ps[:])
            gate_low_t[c] = gate_low_t_sb

        def compute_gate(s):
            c = s // PAIRS_PER_CHUNK
            first_tile = (s % PAIRS_PER_CHUNK) * PAIR_TILES
            gate_sb = gate_pool.tile([P, PAIR, PACK], F32)
            for i in range(PAIR_TILES):
                tokens = slice((first_tile + i) * P, (first_tile + i + 1) * P)
                z_ps = for_scalar_psum.tile([P, PACK, P], F32, tag="for_scalar")
                for t in range(PACK):
                    nc.tensor.matmul(
                        out=z_ps[:, t, :], lhsT=wg2_by_t[:, t, :], rhs=gate_low_t[c][:, tokens],
                        start=True, stop=True,
                    )
                nc.scalar.activation(
                    out=gate_sb[:, i * P : (i + 1) * P, :],
                    in_=z_ps[:].rearrange("q t n -> q n t"),
                    func=ACT.Sigmoid,
                )
            gate[s] = gate_sb

        def transpose_attn(s):
            first_tile = (s % PAIRS_PER_QUAD) * PAIR_TILES
            attn_t_ps = attn_t_psum.tile([P, 2, PAIR], F32)
            for i in range(PAIR_TILES):
                words = attn_quads[s // PAIRS_PER_QUAD][:, first_tile + i, :].bitcast(F32)
                for u in range(2):
                    nc.tensor.transpose(
                        attn_t_ps[:, u, i * P : (i + 1) * P], words[:, u * P : (u + 1) * P], ident_f32[:]
                    )
            attn_t[s] = attn_t_ps

        def multiply(s):
            quad = s // PAIRS_PER_QUAD
            if s % PAIRS_PER_QUAD == 0:
                h_sb = h_pool.tile([P, QUAD, PACK], BF16, align_bytes=64)
                h[quad] = h_sb
            tokens = slice((s % PAIRS_PER_QUAD) * PAIR, (s % PAIRS_PER_QUAD + 1) * PAIR)
            nc.vector.tensor_tensor(
                out=h[quad][:, tokens, :].rearrange("q n (u e) -> q n u e", e=2),
                in0=attn_t[s][:].bitcast(BF16).rearrange("q u (n e) -> q n u e", e=2),
                in1=gate[s][:].rearrange("q n (u e) -> q n u e", e=2),
                op=ALU.mult,
            )

        def quantise(quad):
            codes = mx_pool.tile([P, QUAD], U32, align_bytes=64)
            scales = mx_pool.tile([P, QUAD], U8, align_bytes=64)
            nc.vector.quantize_mx(
                out=codes[:].bitcast(FP8X4),
                scales=scales[:],
                in_=h[quad][:].rearrange("q n t -> q (n t)"),
            )
            h_codes[quad] = codes
            h_scales[quad] = scales

        def project(quad):
            y_ps = y_psum.tile([P, QUAD_TILES, EO], F32)
            for i in range(QUAD_TILES):
                tokens = slice(i * P, (i + 1) * P)
                nc.tensor.matmul_mx(
                    out=y_ps[:, i, :],
                    lhsT=h_codes[quad][:, tokens].bitcast(FP8X4),
                    lhsT_scale=h_scales[quad][:, tokens],
                    rhs=wo_codes[:].bitcast(FP8X4),
                    rhs_scale=wo_scales[:],
                    start=True,
                    stop=True,
                )
            y[quad] = y_ps

        def statistics(quad):
            stats = stat_pool.tile([P, QUAD_TILES, BN_STATS], F32)
            mean_var_sb = stat_pool.tile([P, QUAD_TILES, BN_AGGR], F32)
            for i in range(QUAD_TILES):
                nc.vector.bn_stats(out=stats[:, i, :], in_=y[quad][:, i, :])
            for i in range(QUAD_TILES):
                nc.vector.bn_aggr(out=mean_var_sb[:, i, :], in_=stats[:, i, :])
            mean_var[quad] = mean_var_sb

        def compute_rstd(quad):
            var_eps = stat_pool.tile([P, QUAD_TILES], F32)
            nc.scalar.activation(
                out=var_eps[:], in_=mean_var[quad][:, :, 1], func=ACT.Identity, bias=LN_EPS, scale=1.0
            )
            rstd_sb = stat_pool.tile([P, QUAD_TILES], F32)
            nc.gpsimd.tensor_tensor(out=rstd_sb[:], in0=var_eps[:], in1=minus_half[:], op=ALU.pow)
            rstd[quad] = rstd_sb
            if not by_vector(quad):
                neg_mean = stat_pool.tile([P, QUAD_TILES], F32)
                nc.scalar.mul(out=neg_mean[:], in_=mean_var[quad][:, :, 0], mul=-1.0)
                shift_sb = stat_pool.tile([P, QUAD_TILES], F32)
                nc.gpsimd.tensor_tensor(out=shift_sb[:], in0=neg_mean[:], in1=rstd_sb[:], op=ALU.mult)
                shift[quad] = shift_sb

        def store(quad, result):
            first_tile = (quad % QUADS_PER_CHUNK) * QUAD_TILES
            nc.sync.dma_start(
                out=chunk_view(out_rows, quad // QUADS_PER_CHUNK)[:, first_tile : first_tile + QUAD_TILES, :],
                in_=result[:],
            )

        def normalise(quad):
            normalised_sb = result_pool.tile([P, QUAD_TILES, EO], F32)
            for i in range(QUAD_TILES):
                nc.scalar.activation(
                    out=normalised_sb[:, i, :], in_=y[quad][:, i, :], func=ACT.Identity,
                    bias=shift[quad][:, i : i + 1], scale=rstd[quad][:, i : i + 1],
                )
            normalised[quad] = normalised_sb

        def scale_and_store(quad):
            result = result_pool.tile([P, QUAD_TILES, EO], F32)
            nc.vector.tensor_tensor(out=result[:], in0=normalised[quad][:], in1=ln_w_quad[:], op=ALU.mult)
            nc.gpsimd.tensor_tensor(out=result[:], in0=result[:], in1=ln_b_quad[:], op=ALU.add)
            store(quad, result)

        def finish_on_vector(quad):
            centred = result_pool.tile([P, QUAD_TILES, EO], F32)
            result = result_pool.tile([P, QUAD_TILES, EO], F32)
            for i in range(QUAD_TILES):
                nc.vector.scalar_tensor_tensor(
                    out=centred[:, i, :], in0=y[quad][:, i, :], scalar=mean_var[quad][:, i, 0:1],
                    in1=ln_w_quad[:, i, :], op0=ALU.subtract, op1=ALU.mult,
                )
            for i in range(QUAD_TILES):
                nc.vector.scalar_tensor_tensor(
                    out=result[:, i, :], in0=centred[:, i, :], scalar=rstd[quad][:, i : i + 1],
                    in1=ln_b_quad[:, i, :], op0=ALU.mult, op1=ALU.add,
                )
            store(quad, result)

        def pair_due(step, lag):
            s = step - lag
            return s if 0 <= s < N_PAIRS else None

        def quad_due(step, lag):
            quad, rest = divmod(step - lag, PAIRS_PER_QUAD)
            return quad if rest == 0 and 0 <= quad < N_QUADS else None

        with tc.manual_schedule():
            transpose_gate_low(0)
            for step in range(N_PAIRS + SCALE_LAG):
                s = pair_due(step, 0)
                if s is not None:
                    compute_gate(s)
                    transpose_attn(s)
                ahead = pair_due(step, -GATE_LOW_LEAD)
                if ahead is not None and ahead % PAIRS_PER_CHUNK == 0:
                    transpose_gate_low(ahead // PAIRS_PER_CHUNK)
                quad = quad_due(step, PROJECT_LAG)
                if quad is not None:
                    project(quad)
                quad = quad_due(step, RSTD_LAG)
                if quad is not None:
                    compute_rstd(quad)
                s = pair_due(step, MULTIPLY_LAG)
                if s is not None:
                    multiply(s)
                if step == QUANTISE_LAG:
                    quantise_wo()
                    spread_ln_w_and_b()
                quad = quad_due(step, QUANTISE_LAG)
                if quad is not None:
                    quantise(quad)
                quad = quad_due(step, STATS_LAG)
                if quad is not None:
                    statistics(quad)
                quad = quad_due(step, SCALE_LAG)
                if quad is not None and not by_vector(quad):
                    scale_and_store(quad)
                quad = quad_due(step, NORMALISE_LAG)
                if quad is not None:
                    if by_vector(quad):
                        finish_on_vector(quad)
                    else:
                        normalise(quad)
